import numpy as np
import ml_dtypes


def mxq(x, axis, fmt="e4m3"):
    dtype, down = {"e4m3": (ml_dtypes.float8_e4m3fn, 7), "e5m2": (ml_dtypes.float8_e5m2, 14)}[fmt]
    v = np.moveaxis(np.asarray(x, np.float32).astype(ml_dtypes.bfloat16).astype(np.float64), axis, -1)
    blocks = v.reshape(v.shape[:-1] + (-1, 32))
    amax = np.abs(blocks).max(-1, keepdims=True)
    byte = np.maximum(np.where(amax > 0, np.frexp(amax)[1] - 1 + 127, 0) - down, 1)
    scale = np.exp2(byte - 127.0)
    codes = (blocks / scale).astype(np.float32).astype(dtype).astype(np.float64)
    return np.moveaxis((codes * scale).reshape(v.shape), -1, axis)


WIDE = False


def mx_kscale(k):
    if not WIDE:
        return np.ones(k)
    levels = np.array([10, -10, 5, -5, 0])
    a = np.random.permutation(np.resize(levels, k // 512 * 4)).reshape(k // 512, 4)
    idx = np.arange(k)
    return np.exp2(a[idx // 512, idx % 128 // 32])


BF16 = ml_dtypes.bfloat16


def bf(x):
    return np.asarray(x, np.float32).astype(BF16)


def f64(x):
    return np.asarray(x).astype(np.float64)


NS, NT, DS, DT, DH, DB, DO, NF, SP = 4096, 1024, 1024, 128, 1024, 256, 512, 2, 16
EPS_ROW = 1e-8
EPS_BN = 1e-5


def row_norm(a):
    return a / np.maximum(a.sum(axis=1, keepdims=True), EPS_ROW)


def bn_eval(x, gamma, beta, mean, var):
    return (x - mean) * (gamma / np.sqrt(var + EPS_BN)) + beta


def setup_inputs():
    t = mx_kscale(DH)
    edges = np.random.random((NT, NS)) < 1.0 / SP
    linked = np.random.random((1, NS)) > 0.03
    return {"h_tgt": bf(np.maximum(np.random.standard_normal((NT, DH)) * 1.25, 0.0) * t),
            "A": bf(np.random.random((NT, NS)) * edges * linked),
            "Wb0": bf(np.random.standard_normal((DH, DB)) * 4.0 / np.sqrt(DH) / t[:, None]),
            "bb0": bf(np.random.standard_normal(DB) * 0.1),
            "bn_b_gamma": bf(np.random.uniform(0.5, 1.5, DB)),
            "bn_b_beta": bf(np.random.standard_normal(DB) * 0.1),
            "bn_b_mean": bf(np.random.standard_normal(DB) * 0.1),
            "bn_b_var": bf(np.random.uniform(0.5, 1.5, DB))}


def reference(h_tgt, A, Wb0, bb0, bn_b_gamma, bn_b_beta, bn_b_mean, bn_b_var):
    at_n = row_norm(f64(A).T)
    agg = mxq(at_n, 1, "e4m3") @ mxq(f64(h_tgt), 0, "e4m3")
    h = (mxq(agg, 1, "e4m3") @ mxq(f64(Wb0), 0, "e4m3")) + f64(bb0)
    return np.maximum(bn_eval(h, f64(bn_b_gamma), f64(bn_b_beta), f64(bn_b_mean), f64(bn_b_var)), 0.0)

@@ -1,0 +1,309 @@
+from contextlib import ExitStack
+
+import concourse.mybir as mybir
+from concourse.masks import make_identity
+
+F32 = mybir.dt.float32
+BF16 = mybir.dt.bfloat16
+U32 = mybir.dt.uint32
+U8 = mybir.dt.uint8
+FP8X4 = mybir.dt.float8_e4m3fn_x4
+ALU = mybir.AluOpType
+ACT = mybir.ActivationFunctionType
+
+NT, NS, DH, DB = 1024, 4096, 1024, 256
+EPS_ROW = 1e-8
+EPS_BN = 1e-5
+
+P = 128
+PACK = 4
+K_PASS = P * PACK
+T_PASSES = NT // K_PASS
+F_PASSES = DH // K_PASS
+D_TILES = DB // P
+
+SB = 512
+ST = SB // P
+NB = NS // SB
+SUM_COLS = 32
+RUN = 4
+
+FLOPS = 2 * NS * NT * DH + 2 * NS * DH * DB
+
+
+def tile_bipartitegcnstack_pb_t_kernel(
+    tc, h_tgt, A, Wb0, bb0, bn_b_gamma, bn_b_beta, bn_b_mean, bn_b_var, out
+):
+    nc = tc.nc
+    with ExitStack() as ctx:
+        ctx.enter_context(tc.manual_schedule())
+
+        consts = ctx.enter_context(tc.tile_pool(name="consts", bufs=1))
+        small = ctx.enter_context(tc.tile_pool(name="small", bufs=4))
+        a_pool = ctx.enter_context(tc.tile_pool(name="a_pool", bufs=NB))
+        h_pool = ctx.enter_context(tc.tile_pool(name="h_pool", bufs=T_PASSES))
+        hq_pool = ctx.enter_context(tc.tile_pool(name="hq_pool", bufs=F_PASSES * T_PASSES))
+        w_pool = ctx.enter_context(tc.tile_pool(name="w_pool", bufs=1))
+        an_pool = ctx.enter_context(tc.tile_pool(name="an_pool", bufs=2 * T_PASSES))
+        aq_pool = ctx.enter_context(tc.tile_pool(name="aq_pool", bufs=3 * T_PASSES))
+        gg_pool = ctx.enter_context(tc.tile_pool(name="gg_pool", bufs=3))
+        gq_pool = ctx.enter_context(tc.tile_pool(name="gq_pool", bufs=2 * F_PASSES))
+        act_pool = ctx.enter_context(tc.tile_pool(name="act_pool", bufs=2 * D_TILES))
+        out_pool = ctx.enter_context(tc.tile_pool(name="out_pool", bufs=2))
+        psum_sum = ctx.enter_context(tc.psum_pool(name="psum_sum", bufs=1))
+        psum_inv = ctx.enter_context(tc.psum_pool(name="psum_inv", bufs=2))
+        psum_agg = ctx.enter_context(tc.psum_pool(name="psum_agg", bufs=3))
+        psum_post = ctx.enter_context(tc.psum_pool(name="psum_post", bufs=2))
+
+        a_raw, h_raw = {}, {}
+        sums, inv, inv_all = {}, {}, {}
+        a_grp, h_grp, agg_grp = {}, {}, {}
+        a_q, h_q, agg_q = {}, {}, {}
+        act_t = {}
+
+        def regroup(copy, grouped, rows):
+            copy(
+                out=grouped.rearrange("p (q i) j -> p q j i", i=RUN),
+                in_=rows.rearrange("p j (q i) -> p q j i", i=RUN),
+            )
+
+        def quantise(pool, label, grouped):
+            width = grouped.shape[1]
+            codes = pool.tile([P, width], U32, name=label + "_codes", align_bytes=64)
+            scales = pool.tile([P, width], U8, name=label + "_scales", align_bytes=64)
+            nc.vector.quantize_mx(
+                out=codes[:].bitcast(FP8X4),
+                scales=scales[:],
+                in_=grouped[:].rearrange("p w j -> p (w j)"),
+            )
+            return codes, scales
+
+        def load_a(b):
+            a_raw[b] = a_pool.tile([P, T_PASSES, PACK, SB], BF16, name="a_raw")
+            for c in range(T_PASSES):
+                rows = A[c * K_PASS : (c + 1) * K_PASS, b * SB : (b + 1) * SB]
+                nc.sync.dma_start(
+                    out=a_raw[b][:, c], in_=rows.rearrange("(p j) s -> p j s", j=PACK)
+                )
+
+        def load_h(c):
+            h_raw[c] = h_pool.tile([P, PACK, DH], BF16, name="h_raw")
+            rows = h_tgt[c * K_PASS : (c + 1) * K_PASS, :]
+            nc.sync.dma_start(out=h_raw[c][:], in_=rows.rearrange("(p j) f -> p j f", j=PACK))
+
+        def column_sums(b):
+            sums[b] = psum_sum.tile([P, ST, SUM_COLS], F32, name="sums")
+            pieces = T_PASSES * PACK
+            for st in range(ST):
+                for r in range(pieces):
+                    nc.tensor.matmul(
+                        out=sums[b][:, st, :],
+                        lhsT=a_raw[b][:, r // PACK, r % PACK, st * P : (st + 1) * P],
+                        rhs=ones[:],
+                        start=(r == 0),
+                        stop=(r == pieces - 1),
+                    )
+
+        def reciprocals(b):
+            clamped = small.tile([P, ST], F32, name="clamped")
+            nc.vector.tensor_scalar_max(out=clamped[:], in0=sums[b][:, :, 0], scalar1=EPS_ROW)
+            inv[b] = small.tile([P, ST], F32, name="inv")
+            nc.vector.reciprocal(out=inv[b][:], in_=clamped[:])
+
+        def spread(b):
+            inv_all[b] = psum_inv.tile([P, SB], F32, name="inv_all")
+            for st in range(ST):
+                nc.tensor.transpose(
+                    out=inv_all[b][:, st * P : (st + 1) * P],
+                    in_=inv[b][:, st : st + 1].to_broadcast([P, P]),
+                    identity=ident[:],
+                )
+
+        def normalise(b, c):
+            a_grp[(b, c)] = an_pool.tile([P, SB, PACK], BF16, name="a_grp", align_bytes=64)
+            nc.vector.tensor_tensor(
+                out=a_grp[(b, c)][:],
+                in0=a_raw[b][:, c].rearrange("p j s -> p s j"),
+                in1=inv_all[b][:].unsqueeze(2).to_broadcast([P, SB, PACK]),
+                op=ALU.mult,
+            )
+
+        def quantise_a(b, c):
+            a_q[(b, c)] = quantise(aq_pool, "a", a_grp[(b, c)])
+
+        def aggregate(b, g):
+            agg_grp[(b, g)] = gg_pool.tile([P, SB, PACK], BF16, name="agg_grp", align_bytes=64)
+            for st in range(ST):
+                nodes = slice(st * P, (st + 1) * P)
+                bank = psum_agg.tile([P, PACK, P], F32, name="agg_bank")
+                for i in range(PACK):
+                    feats = slice(i * P, (i + 1) * P)
+                    for c in range(T_PASSES):
+                        h_codes, h_scales = h_q[(g, c)]
+                        a_codes, a_scales = a_q[(b, c)]
+                        nc.tensor.matmul_mx(
+                            out=bank[:, i, :],
+                            lhsT=h_codes[:, feats].bitcast(FP8X4),
+                            lhsT_scale=h_scales[:, feats],
+                            rhs=a_codes[:, nodes].bitcast(FP8X4),
+                            rhs_scale=a_scales[:, nodes],
+                            start=(c == 0),
+                            stop=(c == T_PASSES - 1),
+                        )
+                nc.scalar.copy(
+                    out=agg_grp[(b, g)][:, nodes, :], in_=bank[:].rearrange("p i s -> p s i")
+                )
+
+        def quantise_agg(b, g):
+            agg_q[(b, g)] = quantise(gq_pool, "agg", agg_grp[(b, g)])
+
+        def project(b, dt):
+            bank = psum_post.tile([P, SB], F32, name="proj_bank", tag="post")
+            w_codes, w_scales = w_q
+            for g in range(F_PASSES):
+                cols = slice(g * DB + dt * P, g * DB + (dt + 1) * P)
+                agg_codes, agg_scales = agg_q[(b, g)]
+                nc.tensor.matmul_mx(
+                    out=bank[:],
+                    lhsT=w_codes[:, cols].bitcast(FP8X4),
+                    lhsT_scale=w_scales[:, cols],
+                    rhs=agg_codes[:].bitcast(FP8X4),
+                    rhs_scale=agg_scales[:],
+                    start=(g == 0),
+                    stop=(g == F_PASSES - 1),
+                )
+            act_t[(b, dt)] = act_pool.tile([P, SB], F32, name="act_t")
+            nc.scalar.activation(
+                out=act_t[(b, dt)][:],
+                in_=bank[:],
+                func=ACT.Relu,
+                bias=bn_shift[:, dt : dt + 1],
+                scale=bn_scale[:, dt : dt + 1],
+            )
+
+        def turn_and_store(b):
+            rows = out_pool.tile([P, ST, DB], F32, name="rows")
+            for pair in range(ST // 2):
+                bank = psum_post.tile([P, 2, DB], F32, name="turn_bank", tag="post")
+                for k in range(2):
+                    nodes = slice((2 * pair + k) * P, (2 * pair + k + 1) * P)
+                    for dt in range(D_TILES):
+                        nc.tensor.transpose(
+                            out=bank[:, k, dt * P : (dt + 1) * P],
+                            in_=act_t[(b, dt)][:, nodes],
+                            identity=ident[:],
+                        )
+                nc.scalar.copy(out=rows[:, 2 * pair : 2 * pair + 2, :], in_=bank[:])
+            nc.sync.dma_start(
+                out=out[b * SB : (b + 1) * SB, :].rearrange("(st p) d -> p st d", p=P),
+                in_=rows[:],
+            )
+
+        ident = consts.tile([P, P], F32, name="ident")
+        make_identity(nc, ident[:])
+        ones = consts.tile([P, SUM_COLS], BF16, name="ones")
+        nc.vector.memset(ones[:], 1.0)
+
+        vectors = [bb0, bn_b_gamma, bn_b_beta, bn_b_mean, bn_b_var]
+        vec_rows = consts.tile([P, P], BF16, name="vec_rows")
+        nc.vector.memset(vec_rows[:], 0.0)
+        for v in range(len(vectors)):
+            nc.scalar.dma_start(
+                out=vec_rows[v * D_TILES : (v + 1) * D_TILES, :],
+                in_=vectors[v].rearrange("(dt d) -> dt d", dt=D_TILES),
+            )
+
+        load_a(0)
+        load_h(0)
+        load_h(1)
+        load_a(1)
+        w_raw = w_pool.tile([P, F_PASSES * PACK, DB], BF16, name="w_raw")
+        nc.sync.dma_start(out=w_raw[:], in_=Wb0.rearrange("(gi p) d -> p gi d", p=P))
+        for b in range(2, NB):
+            load_a(b)
+
+        vec_f32 = consts.tile([P, P], F32, name="vec_f32")
+        nc.vector.tensor_copy(out=vec_f32[:], in_=vec_rows[:])
+        vec_bank = psum_post.tile([P, P], F32, name="vec_bank", tag="post")
+        nc.tensor.transpose(out=vec_bank[:], in_=vec_f32[:], identity=ident[:])
+        vec_t = consts.tile([P, len(vectors), D_TILES], F32, name="vec_t")
+        nc.vector.tensor_copy(
+            out=vec_t[:].rearrange("p v dt -> p (v dt)"), in_=vec_bank[:, 0 : len(vectors) * D_TILES]
+        )
+        bias_t, gamma_t, beta_t, mean_t, var_t = [vec_t[:, v, :] for v in range(len(vectors))]
+        var_eps = consts.tile([P, D_TILES], F32, name="var_eps")
+        nc.vector.tensor_scalar_add(out=var_eps[:], in0=var_t, scalar1=EPS_BN)
+        std = consts.tile([P, D_TILES], F32, name="std")
+        nc.scalar.sqrt(out=std[:], in_=var_eps[:])
+        rstd = consts.tile([P, D_TILES], F32, name="rstd")
+        nc.vector.reciprocal(out=rstd[:], in_=std[:])
+        bn_scale = consts.tile([P, D_TILES], F32, name="bn_scale")
+        nc.vector.tensor_mul(out=bn_scale[:], in0=gamma_t, in1=rstd[:])
+        centred = consts.tile([P, D_TILES], F32, name="centred")
+        nc.vector.tensor_sub(out=centred[:], in0=bias_t, in1=mean_t)
+        scaled = consts.tile([P, D_TILES], F32, name="scaled")
+        nc.vector.tensor_mul(out=scaled[:], in0=centred[:], in1=bn_scale[:])
+        bn_shift = consts.tile([P, D_TILES], F32, name="bn_shift")
+        nc.vector.tensor_add(out=bn_shift[:], in0=scaled[:], in1=beta_t)
+
+        column_sums(0)
+        reciprocals(0)
+        spread(0)
+
+        w_grp = w_pool.tile([P, F_PASSES * DB, PACK], BF16, name="w_grp", align_bytes=64)
+        for g in range(F_PASSES):
+            for c in range(T_PASSES):
+                h_grp[(g, c)] = hq_pool.tile([P, K_PASS, PACK], BF16, name="h_grp", align_bytes=64)
+                first = g == 0 and c == 0
+                regroup(
+                    nc.vector.tensor_copy if first else nc.scalar.copy,
+                    h_grp[(g, c)][:],
+                    h_raw[c][:, :, g * K_PASS : (g + 1) * K_PASS],
+                )
+        for g in range(F_PASSES):
+            regroup(
+                nc.scalar.copy,
+                w_grp[:, g * DB : (g + 1) * DB, :],
+                w_raw[:, g * PACK : (g + 1) * PACK, :],
+            )
+
+        for c in range(T_PASSES):
+            normalise(0, c)
+        for c in range(T_PASSES):
+            h_q[(0, c)] = quantise(hq_pool, "h", h_grp[(0, c)])
+        column_sums(1)
+        reciprocals(1)
+        spread(1)
+        for c in range(T_PASSES):
+            quantise_a(0, c)
+        for c in range(T_PASSES):
+            h_q[(1, c)] = quantise(hq_pool, "h", h_grp[(1, c)])
+        w_q = quantise(w_pool, "w", w_grp)
+
+        for b in range(NB + 1):
+            if b >= 1:
+                quantise_agg(b - 1, 1)
+            if b < NB:
+                aggregate(b, 0)
+            if b + 1 < NB:
+                normalise(b + 1, 0)
+                normalise(b + 1, 1)
+            if b >= 1:
+                project(b - 1, 0)
+            if b + 2 < NB:
+                column_sums(b + 2)
+                reciprocals(b + 2)
+            if b >= 1:
+                project(b - 1, 1)
+            if b + 1 < NB:
+                quantise_a(b + 1, 0)
+            if b < NB:
+                quantise_agg(b, 0)
+            if b + 1 < NB:
+                quantise_a(b + 1, 1)
+            if b < NB:
+                aggregate(b, 1)
+            if b + 2 < NB:
+                spread(b + 2)
+            if b >= 1:
+                turn_and_store(b - 1)

@@ -201,6 +201,8 @@ def tile_bipartitegcnstack_pb_t_kernel(
 
         ident = consts.tile([P, P], F32, name="ident")
         make_identity(nc, ident[:])
+        ident_bf = consts.tile([P, P], BF16, name="ident_bf")
+        make_identity(nc, ident_bf[:])
         ones = consts.tile([P, SUM_COLS], BF16, name="ones")
         nc.vector.memset(ones[:], 1.0)
 
@@ -222,33 +224,25 @@ def tile_bipartitegcnstack_pb_t_kernel(
         for b in range(2, NB):
             load_a(b)
 
-        vec_f32 = consts.tile([P, P], F32, name="vec_f32")
-        nc.vector.tensor_copy(out=vec_f32[:], in_=vec_rows[:])
-        vec_bank = psum_post.tile([P, P], F32, name="vec_bank", tag="post")
-        nc.tensor.transpose(out=vec_bank[:], in_=vec_f32[:], identity=ident[:])
-        vec_t = consts.tile([P, len(vectors), D_TILES], F32, name="vec_t")
-        nc.vector.tensor_copy(
-            out=vec_t[:].rearrange("p v dt -> p (v dt)"), in_=vec_bank[:, 0 : len(vectors) * D_TILES]
-        )
-        bias_t, gamma_t, beta_t, mean_t, var_t = [vec_t[:, v, :] for v in range(len(vectors))]
-        var_eps = consts.tile([P, D_TILES], F32, name="var_eps")
-        nc.vector.tensor_scalar_add(out=var_eps[:], in0=var_t, scalar1=EPS_BN)
-        std = consts.tile([P, D_TILES], F32, name="std")
-        nc.scalar.sqrt(out=std[:], in_=var_eps[:])
-        rstd = consts.tile([P, D_TILES], F32, name="rstd")
-        nc.vector.reciprocal(out=rstd[:], in_=std[:])
-        bn_scale = consts.tile([P, D_TILES], F32, name="bn_scale")
-        nc.vector.tensor_mul(out=bn_scale[:], in0=gamma_t, in1=rstd[:])
-        centred = consts.tile([P, D_TILES], F32, name="centred")
-        nc.vector.tensor_sub(out=centred[:], in0=bias_t, in1=mean_t)
-        scaled = consts.tile([P, D_TILES], F32, name="scaled")
-        nc.vector.tensor_mul(out=scaled[:], in0=centred[:], in1=bn_scale[:])
-        bn_shift = consts.tile([P, D_TILES], F32, name="bn_shift")
-        nc.vector.tensor_add(out=bn_shift[:], in0=scaled[:], in1=beta_t)
-
         column_sums(0)
         reciprocals(0)
         spread(0)
+
+        vec_bank = psum_post.tile([P, P], BF16, name="vec_bank", tag="post")
+        nc.tensor.transpose(out=vec_bank[:], in_=vec_rows[:], identity=ident_bf[:])
+        kept = len(vectors) - 1
+        vec_t = consts.tile([P, kept, D_TILES], F32, name="vec_t")
+        nc.scalar.copy(
+            out=vec_t[:].rearrange("p v dt -> p (v dt)"), in_=vec_bank[:, 0 : kept * D_TILES]
+        )
+        bias_t, gamma_t, beta_t, mean_t = [vec_t[:, v, :] for v in range(kept)]
+        std = consts.tile([P, D_TILES], F32, name="std")
+        nc.scalar.activation(
+            out=std[:],
+            in_=vec_bank[:, kept * D_TILES : (kept + 1) * D_TILES],
+            func=ACT.Sqrt,
+            bias=EPS_BN,
+        )
 
         w_grp = w_pool.tile([P, F_PASSES * DB, PACK], BF16, name="w_grp", align_bytes=64)
         for g in range(F_PASSES):
@@ -269,6 +263,16 @@ def tile_bipartitegcnstack_pb_t_kernel(
 
         for c in range(T_PASSES):
             normalise(0, c)
+        rstd = consts.tile([P, D_TILES], F32, name="rstd")
+        nc.vector.reciprocal(out=rstd[:], in_=std[:])
+        bn_scale = consts.tile([P, D_TILES], F32, name="bn_scale")
+        nc.gpsimd.tensor_tensor(out=bn_scale[:], in0=gamma_t, in1=rstd[:], op=ALU.mult)
+        centred = consts.tile([P, D_TILES], F32, name="centred")
+        nc.gpsimd.tensor_tensor(out=centred[:], in0=bias_t, in1=mean_t, op=ALU.subtract)
+        scaled = consts.tile([P, D_TILES], F32, name="scaled")
+        nc.gpsimd.tensor_tensor(out=scaled[:], in0=centred[:], in1=bn_scale[:], op=ALU.mult)
+        bn_shift = consts.tile([P, D_TILES], F32, name="bn_shift")
+        nc.gpsimd.tensor_tensor(out=bn_shift[:], in0=scaled[:], in1=beta_t, op=ALU.add)
         for c in range(T_PASSES):
             h_q[(0, c)] = quantise(hq_pool, "h", h_grp[(0, c)])
         column_sums(1)

@@ -25,6 +25,8 @@ D_TILES = DB // P
 SB = 512
 ST = SB // P
 NB = NS // SB
+HB = SB // 2
+HT = HB // P
 SUM_COLS = 32
 RUN = 4
 
@@ -44,12 +46,12 @@ def tile_bipartitegcnstack_pb_t_kernel(
         h_pool = ctx.enter_context(tc.tile_pool(name="h_pool", bufs=T_PASSES))
         hq_pool = ctx.enter_context(tc.tile_pool(name="hq_pool", bufs=F_PASSES * T_PASSES))
         w_pool = ctx.enter_context(tc.tile_pool(name="w_pool", bufs=1))
-        an_pool = ctx.enter_context(tc.tile_pool(name="an_pool", bufs=2 * T_PASSES))
-        aq_pool = ctx.enter_context(tc.tile_pool(name="aq_pool", bufs=3 * T_PASSES))
+        an_pool = ctx.enter_context(tc.tile_pool(name="an_pool", bufs=3))
+        aq_pool = ctx.enter_context(tc.tile_pool(name="aq_pool", bufs=4))
         gg_pool = ctx.enter_context(tc.tile_pool(name="gg_pool", bufs=3))
-        gq_pool = ctx.enter_context(tc.tile_pool(name="gq_pool", bufs=2 * F_PASSES))
+        gq_pool = ctx.enter_context(tc.tile_pool(name="gq_pool", bufs=4))
         act_pool = ctx.enter_context(tc.tile_pool(name="act_pool", bufs=2 * D_TILES))
-        out_pool = ctx.enter_context(tc.tile_pool(name="out_pool", bufs=2))
+        out_pool = ctx.enter_context(tc.tile_pool(name="out_pool", bufs=4))
         psum_sum = ctx.enter_context(tc.psum_pool(name="psum_sum", bufs=1))
         psum_inv = ctx.enter_context(tc.psum_pool(name="psum_inv", bufs=2))
         psum_agg = ctx.enter_context(tc.psum_pool(name="psum_agg", bufs=3))
@@ -57,8 +59,9 @@ def tile_bipartitegcnstack_pb_t_kernel(
 
         a_raw, h_raw = {}, {}
         sums, inv, inv_all = {}, {}, {}
-        a_grp, h_grp, agg_grp = {}, {}, {}
-        a_q, h_q, agg_q = {}, {}, {}
+        a_grp, agg_grp = {}, {}
+        h_grp = {}
+        a_q, agg_q, h_q = {}, {}, {}
         act_t = {}
 
         def regroup(copy, grouped, rows):
@@ -91,6 +94,13 @@ def tile_bipartitegcnstack_pb_t_kernel(
             rows = h_tgt[c * K_PASS : (c + 1) * K_PASS, :]
             nc.sync.dma_start(out=h_raw[c][:], in_=rows.rearrange("(p j) f -> p j f", j=PACK))
 
+        def regroup_h(copy, g, c):
+            h_grp[(g, c)] = hq_pool.tile([P, K_PASS, PACK], BF16, name="h_grp", align_bytes=64)
+            regroup(copy, h_grp[(g, c)][:], h_raw[c][:, :, g * K_PASS : (g + 1) * K_PASS])
+
+        def quantise_h(g, c):
+            h_q[(g, c)] = quantise(hq_pool, "h", h_grp[(g, c)])
+
         def column_sums(b):
             sums[b] = psum_sum.tile([P, ST, SUM_COLS], F32, name="sums")
             pieces = T_PASSES * PACK
@@ -119,59 +129,71 @@ def tile_bipartitegcnstack_pb_t_kernel(
                     identity=ident[:],
                 )
 
-        def normalise(b, c):
-            a_grp[(b, c)] = an_pool.tile([P, SB, PACK], BF16, name="a_grp", align_bytes=64)
+        def normalise(b, half):
+            nodes = slice(half * HB, (half + 1) * HB)
+            a_grp[(b, half)] = an_pool.tile(
+                [P, T_PASSES * HB, PACK], BF16, name="a_grp", align_bytes=64
+            )
             nc.vector.tensor_tensor(
-                out=a_grp[(b, c)][:],
-                in0=a_raw[b][:, c].rearrange("p j s -> p s j"),
-                in1=inv_all[b][:].unsqueeze(2).to_broadcast([P, SB, PACK]),
+                out=a_grp[(b, half)][:].rearrange("p (c s) j -> p c s j", c=T_PASSES),
+                in0=a_raw[b][:, :, :, nodes].rearrange("p c j s -> p c s j"),
+                in1=inv_all[b][:, nodes]
+                .unsqueeze(1)
+                .unsqueeze(3)
+                .to_broadcast([P, T_PASSES, HB, PACK]),
                 op=ALU.mult,
             )
 
-        def quantise_a(b, c):
-            a_q[(b, c)] = quantise(aq_pool, "a", a_grp[(b, c)])
+        def quantise_a(b, half):
+            a_q[(b, half)] = quantise(aq_pool, "a", a_grp[(b, half)])
 
-        def aggregate(b, g):
-            agg_grp[(b, g)] = gg_pool.tile([P, SB, PACK], BF16, name="agg_grp", align_bytes=64)
-            for st in range(ST):
-                nodes = slice(st * P, (st + 1) * P)
-                bank = psum_agg.tile([P, PACK, P], F32, name="agg_bank")
-                for i in range(PACK):
-                    feats = slice(i * P, (i + 1) * P)
-                    for c in range(T_PASSES):
-                        h_codes, h_scales = h_q[(g, c)]
-                        a_codes, a_scales = a_q[(b, c)]
-                        nc.tensor.matmul_mx(
-                            out=bank[:, i, :],
-                            lhsT=h_codes[:, feats].bitcast(FP8X4),
-                            lhsT_scale=h_scales[:, feats],
-                            rhs=a_codes[:, nodes].bitcast(FP8X4),
-                            rhs_scale=a_scales[:, nodes],
-                            start=(c == 0),
-                            stop=(c == T_PASSES - 1),
-                        )
-                nc.scalar.copy(
-                    out=agg_grp[(b, g)][:, nodes, :], in_=bank[:].rearrange("p i s -> p s i")
-                )
+        def aggregate(b, half):
+            agg_grp[(b, half)] = gg_pool.tile(
+                [P, F_PASSES * HB, PACK], BF16, name="agg_grp", align_bytes=64
+            )
+            a_codes, a_scales = a_q[(b, half)]
+            for g in range(F_PASSES):
+                for k in range(HT):
+                    bank = psum_agg.tile([P, PACK, P], F32, name="agg_bank")
+                    for i in range(PACK):
+                        feats = slice(i * P, (i + 1) * P)
+                        for c in range(T_PASSES):
+                            nodes = slice(c * HB + k * P, c * HB + (k + 1) * P)
+                            h_codes, h_scales = h_q[(g, c)]
+                            nc.tensor.matmul_mx(
+                                out=bank[:, i, :],
+                                lhsT=h_codes[:, feats].bitcast(FP8X4),
+                                lhsT_scale=h_scales[:, feats],
+                                rhs=a_codes[:, nodes].bitcast(FP8X4),
+                                rhs_scale=a_scales[:, nodes],
+                                start=(c == 0),
+                                stop=(c == T_PASSES - 1),
+                            )
+                    nc.scalar.copy(
+                        out=agg_grp[(b, half)][:, g * HB + k * P : g * HB + (k + 1) * P, :],
+                        in_=bank[:].rearrange("p i s -> p s i"),
+                    )
 
-        def quantise_agg(b, g):
-            agg_q[(b, g)] = quantise(gq_pool, "agg", agg_grp[(b, g)])
+        def quantise_agg(b, half):
+            agg_q[(b, half)] = quantise(gq_pool, "agg", agg_grp[(b, half)])
 
         def project(b, dt):
             bank = psum_post.tile([P, SB], F32, name="proj_bank", tag="post")
             w_codes, w_scales = w_q
-            for g in range(F_PASSES):
-                cols = slice(g * DB + dt * P, g * DB + (dt + 1) * P)
-                agg_codes, agg_scales = agg_q[(b, g)]
-                nc.tensor.matmul_mx(
-                    out=bank[:],
-                    lhsT=w_codes[:, cols].bitcast(FP8X4),
-                    lhsT_scale=w_scales[:, cols],
-                    rhs=agg_codes[:].bitcast(FP8X4),
-                    rhs_scale=agg_scales[:],
-                    start=(g == 0),
-                    stop=(g == F_PASSES - 1),
-                )
+            for half in range(2):
+                agg_codes, agg_scales = agg_q[(b, half)]
+                for g in range(F_PASSES):
+                    cols = slice(g * DB + dt * P, g * DB + (dt + 1) * P)
+                    nodes = slice(g * HB, (g + 1) * HB)
+                    nc.tensor.matmul_mx(
+                        out=bank[:, half * HB : (half + 1) * HB],
+                        lhsT=w_codes[:, cols].bitcast(FP8X4),
+                        lhsT_scale=w_scales[:, cols],
+                        rhs=agg_codes[:, nodes].bitcast(FP8X4),
+                        rhs_scale=agg_scales[:, nodes],
+                        start=(g == 0),
+                        stop=(g == F_PASSES - 1),
+                    )
             act_t[(b, dt)] = act_pool.tile([P, SB], F32, name="act_t")
             nc.scalar.activation(
                 out=act_t[(b, dt)][:],
@@ -182,7 +204,6 @@ def tile_bipartitegcnstack_pb_t_kernel(
             )
 
         def turn_and_store(b):
-            rows = out_pool.tile([P, ST, DB], F32, name="rows")
             for pair in range(ST // 2):
                 bank = psum_post.tile([P, 2, DB], F32, name="turn_bank", tag="post")
                 for k in range(2):
@@ -193,11 +214,13 @@ def tile_bipartitegcnstack_pb_t_kernel(
                             in_=act_t[(b, dt)][:, nodes],
                             identity=ident[:],
                         )
-                nc.scalar.copy(out=rows[:, 2 * pair : 2 * pair + 2, :], in_=bank[:])
-            nc.sync.dma_start(
-                out=out[b * SB : (b + 1) * SB, :].rearrange("(st p) d -> p st d", p=P),
-                in_=rows[:],
-            )
+                rows = out_pool.tile([P, 2, DB], F32, name="rows")
+                nc.scalar.copy(out=rows[:], in_=bank[:])
+                first = b * SB + 2 * pair * P
+                nc.sync.dma_start(
+                    out=out[first : first + 2 * P, :].rearrange("(k p) d -> p k d", p=P),
+                    in_=rows[:],
+                )
 
         ident = consts.tile([P, P], F32, name="ident")
         make_identity(nc, ident[:])
@@ -227,9 +250,22 @@ def tile_bipartitegcnstack_pb_t_kernel(
         column_sums(0)
         reciprocals(0)
         spread(0)
-
         vec_bank = psum_post.tile([P, P], BF16, name="vec_bank", tag="post")
         nc.tensor.transpose(out=vec_bank[:], in_=vec_rows[:], identity=ident_bf[:])
+
+        regroup_h(nc.vector.tensor_copy, 0, 0)
+        regroup_h(nc.scalar.copy, 1, 0)
+        regroup_h(nc.scalar.copy, 1, 1)
+        normalise(0, 0)
+        regroup_h(nc.vector.tensor_copy, 0, 1)
+        quantise_h(0, 0)
+        quantise_h(0, 1)
+        quantise_a(0, 0)
+        quantise_h(1, 0)
+        quantise_h(1, 1)
+        column_sums(1)
+        reciprocals(1)
+
         kept = len(vectors) - 1
         vec_t = consts.tile([P, kept, D_TILES], F32, name="vec_t")
         nc.scalar.copy(
@@ -243,26 +279,6 @@ def tile_bipartitegcnstack_pb_t_kernel(
             func=ACT.Sqrt,
             bias=EPS_BN,
         )
-
-        w_grp = w_pool.tile([P, F_PASSES * DB, PACK], BF16, name="w_grp", align_bytes=64)
-        for g in range(F_PASSES):
-            for c in range(T_PASSES):
-                h_grp[(g, c)] = hq_pool.tile([P, K_PASS, PACK], BF16, name="h_grp", align_bytes=64)
-                first = g == 0 and c == 0
-                regroup(
-                    nc.vector.tensor_copy if first else nc.scalar.copy,
-                    h_grp[(g, c)][:],
-                    h_raw[c][:, :, g * K_PASS : (g + 1) * K_PASS],
-                )
-        for g in range(F_PASSES):
-            regroup(
-                nc.scalar.copy,
-                w_grp[:, g * DB : (g + 1) * DB, :],
-                w_raw[:, g * PACK : (g + 1) * PACK, :],
-            )
-
-        for c in range(T_PASSES):
-            normalise(0, c)
         rstd = consts.tile([P, D_TILES], F32, name="rstd")
         nc.vector.reciprocal(out=rstd[:], in_=std[:])
         bn_scale = consts.tile([P, D_TILES], F32, name="bn_scale")
@@ -273,41 +289,40 @@ def tile_bipartitegcnstack_pb_t_kernel(
         nc.gpsimd.tensor_tensor(out=scaled[:], in0=centred[:], in1=bn_scale[:], op=ALU.mult)
         bn_shift = consts.tile([P, D_TILES], F32, name="bn_shift")
         nc.gpsimd.tensor_tensor(out=bn_shift[:], in0=scaled[:], in1=beta_t, op=ALU.add)
-        for c in range(T_PASSES):
-            h_q[(0, c)] = quantise(hq_pool, "h", h_grp[(0, c)])
-        column_sums(1)
-        reciprocals(1)
-        spread(1)
-        for c in range(T_PASSES):
-            quantise_a(0, c)
-        for c in range(T_PASSES):
-            h_q[(1, c)] = quantise(hq_pool, "h", h_grp[(1, c)])
-        w_q = quantise(w_pool, "w", w_grp)
 
-        for b in range(NB + 1):
-            if b >= 1:
+        w_grp = w_pool.tile([P, F_PASSES * DB, PACK], BF16, name="w_grp", align_bytes=64)
+        for b in range(NB + 2):
+            if b < NB:
+                normalise(b, 1)
+            if 1 <= b <= NB:
                 quantise_agg(b - 1, 1)
             if b < NB:
+                quantise_a(b, 1)
                 aggregate(b, 0)
+            if b == 0:
+                for g in range(F_PASSES):
+                    regroup(
+                        nc.scalar.copy,
+                        w_grp[:, g * DB : (g + 1) * DB, :],
+                        w_raw[:, g * PACK : (g + 1) * PACK, :],
+                    )
+            if b + 1 < NB:
+                spread(b + 1)
+            if b >= 2:
+                turn_and_store(b - 2)
             if b + 1 < NB:
                 normalise(b + 1, 0)
-                normalise(b + 1, 1)
-            if b >= 1:
-                project(b - 1, 0)
             if b + 2 < NB:
                 column_sums(b + 2)
                 reciprocals(b + 2)
-            if b >= 1:
+            if 1 <= b <= NB:
+                project(b - 1, 0)
                 project(b - 1, 1)
-            if b + 1 < NB:
-                quantise_a(b + 1, 0)
             if b < NB:
                 quantise_agg(b, 0)
             if b + 1 < NB:
-                quantise_a(b + 1, 1)
+                quantise_a(b + 1, 0)
+            if b == 0:
+                w_q = quantise(w_pool, "w", w_grp)
             if b < NB:
                 aggregate(b, 1)
-            if b + 2 < NB:
-                spread(b + 2)
-            if b >= 1:
-                turn_and_store(b - 1)

@@ -38,8 +38,6 @@ def tile_bipartitegcnstack_pb_t_kernel(
 ):
     nc = tc.nc
     with ExitStack() as ctx:
-        ctx.enter_context(tc.manual_schedule())
-
         consts = ctx.enter_context(tc.tile_pool(name="consts", bufs=1))
         small = ctx.enter_context(tc.tile_pool(name="small", bufs=4))
         a_pool = ctx.enter_context(tc.tile_pool(name="a_pool", bufs=NB))

@@ -44,15 +44,15 @@ def tile_bipartitegcnstack_pb_t_kernel(
         h_pool = ctx.enter_context(tc.tile_pool(name="h_pool", bufs=T_PASSES))
         hq_pool = ctx.enter_context(tc.tile_pool(name="hq_pool", bufs=F_PASSES * T_PASSES))
         w_pool = ctx.enter_context(tc.tile_pool(name="w_pool", bufs=1))
-        an_pool = ctx.enter_context(tc.tile_pool(name="an_pool", bufs=3))
-        aq_pool = ctx.enter_context(tc.tile_pool(name="aq_pool", bufs=4))
-        gg_pool = ctx.enter_context(tc.tile_pool(name="gg_pool", bufs=3))
-        gq_pool = ctx.enter_context(tc.tile_pool(name="gq_pool", bufs=4))
+        an_pool = ctx.enter_context(tc.tile_pool(name="an_pool", bufs=4))
+        aq_pool = ctx.enter_context(tc.tile_pool(name="aq_pool", bufs=6))
+        gg_pool = ctx.enter_context(tc.tile_pool(name="gg_pool", bufs=4))
+        gq_pool = ctx.enter_context(tc.tile_pool(name="gq_pool", bufs=6))
         act_pool = ctx.enter_context(tc.tile_pool(name="act_pool", bufs=2 * D_TILES))
         out_pool = ctx.enter_context(tc.tile_pool(name="out_pool", bufs=4))
         psum_sum = ctx.enter_context(tc.psum_pool(name="psum_sum", bufs=1))
-        psum_inv = ctx.enter_context(tc.psum_pool(name="psum_inv", bufs=2))
-        psum_agg = ctx.enter_context(tc.psum_pool(name="psum_agg", bufs=3))
+        psum_inv = ctx.enter_context(tc.psum_pool(name="psum_inv", bufs=1))
+        psum_agg = ctx.enter_context(tc.psum_pool(name="psum_agg", bufs=F_PASSES * HT))
         psum_post = ctx.enter_context(tc.psum_pool(name="psum_post", bufs=2))
 
         a_raw, h_raw = {}, {}

@@ -41,7 +41,7 @@ def tile_bipartitegcnstack_pb_t_kernel(
         consts = ctx.enter_context(tc.tile_pool(name="consts", bufs=1))
         small = ctx.enter_context(tc.tile_pool(name="small", bufs=4))
         a_pool = ctx.enter_context(tc.tile_pool(name="a_pool", bufs=NB))
-        h_pool = ctx.enter_context(tc.tile_pool(name="h_pool", bufs=T_PASSES))
+        h_pool = ctx.enter_context(tc.tile_pool(name="h_pool", bufs=F_PASSES * T_PASSES))
         hq_pool = ctx.enter_context(tc.tile_pool(name="hq_pool", bufs=F_PASSES * T_PASSES))
         w_pool = ctx.enter_context(tc.tile_pool(name="w_pool", bufs=1))
         an_pool = ctx.enter_context(tc.tile_pool(name="an_pool", bufs=4))
@@ -54,6 +54,7 @@ def tile_bipartitegcnstack_pb_t_kernel(
         psum_inv = ctx.enter_context(tc.psum_pool(name="psum_inv", bufs=1))
         psum_agg = ctx.enter_context(tc.psum_pool(name="psum_agg", bufs=F_PASSES * HT))
         psum_post = ctx.enter_context(tc.psum_pool(name="psum_post", bufs=2))
+        ctx.enter_context(tc.manual_schedule())
 
         a_raw, h_raw = {}, {}
         sums, inv, inv_all = {}, {}, {}
@@ -79,30 +80,35 @@ def tile_bipartitegcnstack_pb_t_kernel(
             )
             return codes, scales
 
-        def load_a(b):
-            a_raw[b] = a_pool.tile([P, T_PASSES, PACK, SB], BF16, name="a_raw")
+        def load_a(b, first=0, width=SB):
+            if first == 0:
+                a_raw[b] = a_pool.tile([P, T_PASSES, PACK, SB], BF16, name="a_raw")
             for c in range(T_PASSES):
-                rows = A[c * K_PASS : (c + 1) * K_PASS, b * SB : (b + 1) * SB]
+                rows = A[c * K_PASS : (c + 1) * K_PASS, b * SB + first : b * SB + first + width]
                 nc.sync.dma_start(
-                    out=a_raw[b][:, c], in_=rows.rearrange("(p j) s -> p j s", j=PACK)
+                    out=a_raw[b][:, c, :, first : first + width],
+                    in_=rows.rearrange("(p j) s -> p j s", j=PACK),
                 )
 
-        def load_h(c):
-            h_raw[c] = h_pool.tile([P, PACK, DH], BF16, name="h_raw")
-            rows = h_tgt[c * K_PASS : (c + 1) * K_PASS, :]
-            nc.sync.dma_start(out=h_raw[c][:], in_=rows.rearrange("(p j) f -> p j f", j=PACK))
+        def load_h(g, c):
+            h_raw[(g, c)] = h_pool.tile([P, PACK, K_PASS], BF16, name="h_raw")
+            rows = h_tgt[c * K_PASS : (c + 1) * K_PASS, g * K_PASS : (g + 1) * K_PASS]
+            nc.sync.dma_start(
+                out=h_raw[(g, c)][:], in_=rows.rearrange("(p j) f -> p j f", j=PACK)
+            )
 
         def regroup_h(copy, g, c):
             h_grp[(g, c)] = hq_pool.tile([P, K_PASS, PACK], BF16, name="h_grp", align_bytes=64)
-            regroup(copy, h_grp[(g, c)][:], h_raw[c][:, :, g * K_PASS : (g + 1) * K_PASS])
+            regroup(copy, h_grp[(g, c)][:], h_raw[(g, c)][:])
 
         def quantise_h(g, c):
             h_q[(g, c)] = quantise(hq_pool, "h", h_grp[(g, c)])
 
-        def column_sums(b):
-            sums[b] = psum_sum.tile([P, ST, SUM_COLS], F32, name="sums")
+        def column_sums(b, tiles=range(ST)):
+            if tiles[0] == 0:
+                sums[b] = psum_sum.tile([P, ST, SUM_COLS], F32, name="sums", tag="sums")
             pieces = T_PASSES * PACK
-            for st in range(ST):
+            for st in tiles:
                 for r in range(pieces):
                     nc.tensor.matmul(
                         out=sums[b][:, st, :],
@@ -112,15 +118,20 @@ def tile_bipartitegcnstack_pb_t_kernel(
                         stop=(r == pieces - 1),
                     )
 
-        def reciprocals(b):
+        def reciprocals(b, tiles=range(ST)):
+            lo, hi = tiles[0], tiles[-1] + 1
             clamped = small.tile([P, ST], F32, name="clamped")
-            nc.vector.tensor_scalar_max(out=clamped[:], in0=sums[b][:, :, 0], scalar1=EPS_ROW)
-            inv[b] = small.tile([P, ST], F32, name="inv")
-            nc.vector.reciprocal(out=inv[b][:], in_=clamped[:])
+            nc.vector.tensor_scalar_max(
+                out=clamped[:, lo:hi], in0=sums[b][:, lo:hi, 0], scalar1=EPS_ROW
+            )
+            if lo == 0:
+                inv[b] = small.tile([P, ST], F32, name="inv")
+            nc.vector.reciprocal(out=inv[b][:, lo:hi], in_=clamped[:, lo:hi])
 
-        def spread(b):
-            inv_all[b] = psum_inv.tile([P, SB], F32, name="inv_all")
-            for st in range(ST):
+        def spread(b, tiles=range(ST)):
+            if tiles[0] == 0:
+                inv_all[b] = psum_inv.tile([P, SB], F32, name="inv_all", tag="inv_all")
+            for st in tiles:
                 nc.tensor.transpose(
                     out=inv_all[b][:, st * P : (st + 1) * P],
                     in_=inv[b][:, st : st + 1].to_broadcast([P, P]),
@@ -145,14 +156,15 @@ def tile_bipartitegcnstack_pb_t_kernel(
         def quantise_a(b, half):
             a_q[(b, half)] = quantise(aq_pool, "a", a_grp[(b, half)])
 
-        def aggregate(b, half):
-            agg_grp[(b, half)] = gg_pool.tile(
-                [P, F_PASSES * HB, PACK], BF16, name="agg_grp", align_bytes=64
-            )
+        def aggregate(b, half, passes=range(F_PASSES)):
+            if passes[0] == 0:
+                agg_grp[(b, half)] = gg_pool.tile(
+                    [P, F_PASSES * HB, PACK], BF16, name="agg_grp", align_bytes=64
+                )
             a_codes, a_scales = a_q[(b, half)]
-            for g in range(F_PASSES):
+            for g in passes:
                 for k in range(HT):
-                    bank = psum_agg.tile([P, PACK, P], F32, name="agg_bank")
+                    bank = psum_agg.tile([P, PACK, P], F32, name="agg_bank", tag="agg_bank")
                     for i in range(PACK):
                         feats = slice(i * P, (i + 1) * P)
                         for c in range(T_PASSES):
@@ -175,10 +187,19 @@ def tile_bipartitegcnstack_pb_t_kernel(
         def quantise_agg(b, half):
             agg_q[(b, half)] = quantise(gq_pool, "agg", agg_grp[(b, half)])
 
-        def project(b, dt):
-            bank = psum_post.tile([P, SB], F32, name="proj_bank", tag="post")
+        def free_bank(source):
+            pool, tag = {
+                "post": (psum_post, "post"),
+                "agg": (psum_agg, "agg_bank"),
+                "sum": (psum_sum, "sums"),
+                "inv": (psum_inv, "inv_all"),
+            }[source]
+            return pool.tile([P, SB], F32, name="bank_" + source, tag=tag)
+
+        def project(b, dt, halves=range(2), source="post"):
+            bank = free_bank(source)
             w_codes, w_scales = w_q
-            for half in range(2):
+            for half in halves:
                 agg_codes, agg_scales = agg_q[(b, half)]
                 for g in range(F_PASSES):
                     cols = slice(g * DB + dt * P, g * DB + (dt + 1) * P)
@@ -192,33 +213,109 @@ def tile_bipartitegcnstack_pb_t_kernel(
                         start=(g == 0),
                         stop=(g == F_PASSES - 1),
                     )
-            act_t[(b, dt)] = act_pool.tile([P, SB], F32, name="act_t")
+            if halves[0] == 0:
+                act_t[(b, dt)] = act_pool.tile([P, SB], F32, name="act_t")
+            done = slice(halves[0] * HB, (halves[-1] + 1) * HB)
             nc.scalar.activation(
-                out=act_t[(b, dt)][:],
-                in_=bank[:],
+                out=act_t[(b, dt)][:, done],
+                in_=bank[:, done],
                 func=ACT.Relu,
                 bias=bn_shift[:, dt : dt + 1],
                 scale=bn_scale[:, dt : dt + 1],
             )
 
-        def turn_and_store(b):
-            for pair in range(ST // 2):
-                bank = psum_post.tile([P, 2, DB], F32, name="turn_bank", tag="post")
+        def turn_and_store(b, pairs=range(ST // 2), copy=nc.scalar.copy, source="post"):
+            for pair in pairs:
+                bank = free_bank(source)
                 for k in range(2):
                     nodes = slice((2 * pair + k) * P, (2 * pair + k + 1) * P)
                     for dt in range(D_TILES):
                         nc.tensor.transpose(
-                            out=bank[:, k, dt * P : (dt + 1) * P],
+                            out=bank[:, k * DB + dt * P : k * DB + (dt + 1) * P],
                             in_=act_t[(b, dt)][:, nodes],
                             identity=ident[:],
                         )
                 rows = out_pool.tile([P, 2, DB], F32, name="rows")
-                nc.scalar.copy(out=rows[:], in_=bank[:])
+                copy(out=rows[:].rearrange("p k d -> p (k d)"), in_=bank[:])
                 first = b * SB + 2 * pair * P
                 nc.sync.dma_start(
                     out=out[first : first + 2 * P, :].rearrange("(k p) d -> p k d", p=P),
                     in_=rows[:],
                 )
+
+        def aggregate_tile(b, half, k):
+            agg_grp[(b, half, k)] = gg_pool.tile(
+                [P, F_PASSES * P, PACK], BF16, name="agg_grp", align_bytes=64
+            )
+            a_codes, a_scales = a_q[(b, half)]
+            for g in range(F_PASSES):
+                bank = psum_agg.tile([P, PACK, P], F32, name="agg_bank", tag="agg_bank")
+                for i in range(PACK):
+                    feats = slice(i * P, (i + 1) * P)
+                    for c in range(T_PASSES):
+                        nodes = slice(c * HB + k * P, c * HB + (k + 1) * P)
+                        h_codes, h_scales = h_q[(g, c)]
+                        nc.tensor.matmul_mx(
+                            out=bank[:, i, :],
+                            lhsT=h_codes[:, feats].bitcast(FP8X4),
+                            lhsT_scale=h_scales[:, feats],
+                            rhs=a_codes[:, nodes].bitcast(FP8X4),
+                            rhs_scale=a_scales[:, nodes],
+                            start=(c == 0),
+                            stop=(c == T_PASSES - 1),
+                        )
+                nc.scalar.copy(
+                    out=agg_grp[(b, half, k)][:, g * P : (g + 1) * P, :],
+                    in_=bank[:].rearrange("p i s -> p s i"),
+                )
+
+        def quantise_agg_tile(b, half, k):
+            agg_q[(b, half, k)] = quantise(gq_pool, "agg", agg_grp[(b, half, k)])
+
+        def project_tile(b, half, k, sources):
+            banks = [free_bank(source) for source in sources]
+            w_codes, w_scales = w_q
+            agg_codes, agg_scales = agg_q[(b, half, k)]
+            act_k = act_pool.tile([P, D_TILES, P], F32, name="act_k")
+            for dt in range(D_TILES):
+                for g in range(F_PASSES):
+                    cols = slice(g * DB + dt * P, g * DB + (dt + 1) * P)
+                    nodes = slice(g * P, (g + 1) * P)
+                    nc.tensor.matmul_mx(
+                        out=banks[dt][:, 0:P],
+                        lhsT=w_codes[:, cols].bitcast(FP8X4),
+                        lhsT_scale=w_scales[:, cols],
+                        rhs=agg_codes[:, nodes].bitcast(FP8X4),
+                        rhs_scale=agg_scales[:, nodes],
+                        start=(g == 0),
+                        stop=(g == F_PASSES - 1),
+                    )
+            nc.scalar.activation(
+                out=act_k[:, 0, :],
+                in_=banks[0][:, 0:P],
+                func=ACT.Relu,
+                bias=bn_shift[:, 0:1],
+                scale=bn_scale[:, 0:1],
+            )
+            nc.vector.tensor_scalar(
+                out=act_k[:, 1, :],
+                in0=banks[1][:, 0:P],
+                scalar1=bn_scale[:, 1:2],
+                scalar2=bn_shift[:, 1:2],
+                op0=ALU.mult,
+                op1=ALU.add,
+            )
+            return act_k
+
+        def turn_tile(b, half, k, act_k, sources):
+            banks = [free_bank(source) for source in sources]
+            for dt in range(D_TILES):
+                nc.tensor.transpose(out=banks[dt][:, 0:P], in_=act_k[:, dt, :], identity=ident[:])
+            rows = out_pool.tile([P, DB], F32, name="rows_k")
+            nc.scalar.copy(out=rows[:, 0:P], in_=banks[0][:, 0:P])
+            nc.vector.tensor_scalar_max(out=rows[:, P:DB], in0=banks[1][:, 0:P], scalar1=0.0)
+            first = b * SB + (half * HT + k) * P
+            nc.sync.dma_start(out=out[first : first + P, :], in_=rows[:])
 
         ident = consts.tile([P, P], F32, name="ident")
         make_identity(nc, ident[:])
@@ -236,34 +333,35 @@ def tile_bipartitegcnstack_pb_t_kernel(
                 in_=vectors[v].rearrange("(dt d) -> dt d", dt=D_TILES),
             )
 
-        load_a(0)
-        load_h(0)
-        load_h(1)
+        load_h(0, 0)
+        load_a(0, 0, HB)
+        load_h(0, 1)
+        load_h(1, 0)
+        load_h(1, 1)
+        load_a(0, HB, HB)
         load_a(1)
         w_raw = w_pool.tile([P, F_PASSES * PACK, DB], BF16, name="w_raw")
         nc.sync.dma_start(out=w_raw[:], in_=Wb0.rearrange("(gi p) d -> p gi d", p=P))
         for b in range(2, NB):
             load_a(b)
 
-        column_sums(0)
-        reciprocals(0)
-        spread(0)
-        vec_bank = psum_post.tile([P, P], BF16, name="vec_bank", tag="post")
-        nc.tensor.transpose(out=vec_bank[:], in_=vec_rows[:], identity=ident_bf[:])
-
+        warm = consts.tile([P, 1], F32, name="warm")
+        nc.scalar.activation(out=warm[:], in_=ones[:, 0:1], func=ACT.Sqrt)
+        first_half, second_half = range(0, HT), range(HT, ST)
+        pass_0, pass_1 = range(0, 1), range(1, 2)
         regroup_h(nc.vector.tensor_copy, 0, 0)
-        regroup_h(nc.scalar.copy, 1, 0)
-        regroup_h(nc.scalar.copy, 1, 1)
-        normalise(0, 0)
-        regroup_h(nc.vector.tensor_copy, 0, 1)
+        column_sums(0, first_half)
         quantise_h(0, 0)
+        reciprocals(0, first_half)
+        spread(0, first_half)
+        regroup_h(nc.scalar.copy, 0, 1)
+        normalise(0, 0)
+        regroup_h(nc.scalar.copy, 1, 0)
         quantise_h(0, 1)
         quantise_a(0, 0)
-        quantise_h(1, 0)
-        quantise_h(1, 1)
-        column_sums(1)
-        reciprocals(1)
-
+        column_sums(0, second_half)
+        vec_bank = psum_post.tile([P, P], BF16, name="vec_bank", tag="post")
+        nc.tensor.transpose(out=vec_bank[:], in_=vec_rows[:], identity=ident_bf[:])
         kept = len(vectors) - 1
         vec_t = consts.tile([P, kept, D_TILES], F32, name="vec_t")
         nc.scalar.copy(
@@ -277,6 +375,15 @@ def tile_bipartitegcnstack_pb_t_kernel(
             func=ACT.Sqrt,
             bias=EPS_BN,
         )
+        aggregate(0, 0, pass_0)
+        regroup_h(nc.vector.tensor_copy, 1, 1)
+        reciprocals(0, second_half)
+        spread(0, second_half)
+        quantise_h(1, 0)
+        quantise_h(1, 1)
+        column_sums(1)
+        aggregate(0, 0, pass_1)
+        normalise(0, 1)
         rstd = consts.tile([P, D_TILES], F32, name="rstd")
         nc.vector.reciprocal(out=rstd[:], in_=std[:])
         bn_scale = consts.tile([P, D_TILES], F32, name="bn_scale")
@@ -288,22 +395,30 @@ def tile_bipartitegcnstack_pb_t_kernel(
         bn_shift = consts.tile([P, D_TILES], F32, name="bn_shift")
         nc.gpsimd.tensor_tensor(out=bn_shift[:], in0=scaled[:], in1=beta_t, op=ALU.add)
 
+        reciprocals(1)
+        quantise_a(0, 1)
+        spread(1)
         w_grp = w_pool.tile([P, F_PASSES * DB, PACK], BF16, name="w_grp", align_bytes=64)
-        for b in range(NB + 2):
-            if b < NB:
-                normalise(b, 1)
-            if 1 <= b <= NB:
-                quantise_agg(b - 1, 1)
-            if b < NB:
-                quantise_a(b, 1)
-                aggregate(b, 0)
-            if b == 0:
-                for g in range(F_PASSES):
-                    regroup(
-                        nc.scalar.copy,
-                        w_grp[:, g * DB : (g + 1) * DB, :],
-                        w_raw[:, g * PACK : (g + 1) * PACK, :],
-                    )
+        for g in range(F_PASSES):
+            regroup(
+                nc.scalar.copy,
+                w_grp[:, g * DB : (g + 1) * DB, :],
+                w_raw[:, g * PACK : (g + 1) * PACK, :],
+            )
+        normalise(1, 0)
+        column_sums(2)
+        reciprocals(2)
+        quantise_agg(0, 0)
+        quantise_a(1, 0)
+        w_q = quantise(w_pool, "w", w_grp)
+        aggregate(0, 1)
+
+        last = NB - 1
+        for b in range(1, NB):
+            normalise(b, 1)
+            quantise_agg(b - 1, 1)
+            quantise_a(b, 1)
+            aggregate(b, 0)
             if b + 1 < NB:
                 spread(b + 1)
             if b >= 2:
@@ -313,14 +428,23 @@ def tile_bipartitegcnstack_pb_t_kernel(
             if b + 2 < NB:
                 column_sums(b + 2)
                 reciprocals(b + 2)
-            if 1 <= b <= NB:
-                project(b - 1, 0)
-                project(b - 1, 1)
-            if b < NB:
-                quantise_agg(b, 0)
+            project(b - 1, 0, source="post" if b + 2 < NB else "sum")
+            project(b - 1, 1, source="post" if b < last else "inv")
+            quantise_agg(b, 0)
             if b + 1 < NB:
                 quantise_a(b + 1, 0)
-            if b == 0:
-                w_q = quantise(w_pool, "w", w_grp)
-            if b < NB:
+            if b < last:
                 aggregate(b, 1)
+
+        aggregate_tile(last, 1, 0)
+        aggregate_tile(last, 1, 1)
+        quantise_agg_tile(last, 1, 0)
+        project(last, 0, range(0, 1), source="sum")
+        project(last, 1, range(0, 1), source="inv")
+        quantise_agg_tile(last, 1, 1)
+        act_0 = project_tile(last, 1, 0, ["agg", "agg"])
+        turn_and_store(last - 1, copy=nc.vector.tensor_copy)
+        act_1 = project_tile(last, 1, 1, ["agg", "agg"])
+        turn_and_store(last, range(0, 1), source="sum")
+        turn_tile(last, 1, 0, act_0, ["inv", "agg"])
+        turn_tile(last, 1, 1, act_1, ["post", "post"])

@@ -143,15 +143,18 @@ def tile_bipartitegcnstack_pb_t_kernel(
             a_grp[(b, half)] = an_pool.tile(
                 [P, T_PASSES * HB, PACK], BF16, name="a_grp", align_bytes=64
             )
-            nc.vector.tensor_tensor(
-                out=a_grp[(b, half)][:].rearrange("p (c s) j -> p c s j", c=T_PASSES),
-                in0=a_raw[b][:, :, :, nodes].rearrange("p c j s -> p c s j"),
-                in1=inv_all[b][:, nodes]
-                .unsqueeze(1)
-                .unsqueeze(3)
-                .to_broadcast([P, T_PASSES, HB, PACK]),
-                op=ALU.mult,
-            )
+            for c in range(T_PASSES):
+                nc.vector.tensor_tensor(
+                    out=a_grp[(b, half)][:, c * HB : (c + 1) * HB, :].rearrange(
+                        "p (q i) j -> p q j i", i=RUN
+                    ),
+                    in0=a_raw[b][:, c, :, nodes].rearrange("p j (q i) -> p q j i", i=RUN),
+                    in1=inv_all[b][:, nodes]
+                    .rearrange("p (q i) -> p q i", i=RUN)
+                    .unsqueeze(2)
+                    .to_broadcast([P, HB // RUN, PACK, RUN]),
+                    op=ALU.mult,
+                )
 
         def quantise_a(b, half):
             a_q[(b, half)] = quantise(aq_pool, "a", a_grp[(b, half)])

@@ -54,7 +54,6 @@ def tile_bipartitegcnstack_pb_t_kernel(
         psum_inv = ctx.enter_context(tc.psum_pool(name="psum_inv", bufs=1))
         psum_agg = ctx.enter_context(tc.psum_pool(name="psum_agg", bufs=F_PASSES * HT))
         psum_post = ctx.enter_context(tc.psum_pool(name="psum_post", bufs=2))
-        ctx.enter_context(tc.manual_schedule())
 
         a_raw, h_raw = {}, {}
         sums, inv, inv_all = {}, {}, {}

@@ -29,6 +29,7 @@ HB = SB // 2
 HT = HB // P
 SUM_COLS = 32
 RUN = 4
+N_RUN = 2
 
 FLOPS = 2 * NS * NT * DH + 2 * NS * DH * DB
 
@@ -145,13 +146,13 @@ def tile_bipartitegcnstack_pb_t_kernel(
             for c in range(T_PASSES):
                 nc.vector.tensor_tensor(
                     out=a_grp[(b, half)][:, c * HB : (c + 1) * HB, :].rearrange(
-                        "p (q i) j -> p q j i", i=RUN
+                        "p (q i) j -> p q j i", i=N_RUN
                     ),
-                    in0=a_raw[b][:, c, :, nodes].rearrange("p j (q i) -> p q j i", i=RUN),
+                    in0=a_raw[b][:, c, :, nodes].rearrange("p j (q i) -> p q j i", i=N_RUN),
                     in1=inv_all[b][:, nodes]
-                    .rearrange("p (q i) -> p q i", i=RUN)
+                    .rearrange("p (q i) -> p q i", i=N_RUN)
                     .unsqueeze(2)
-                    .to_broadcast([P, HB // RUN, PACK, RUN]),
+                    .to_broadcast([P, HB // N_RUN, PACK, N_RUN]),
                     op=ALU.mult,
                 )
 

from contextlib import ExitStack

import concourse.mybir as mybir
from concourse.masks import make_identity

F32 = mybir.dt.float32
BF16 = mybir.dt.bfloat16
U32 = mybir.dt.uint32
U8 = mybir.dt.uint8
FP8X4 = mybir.dt.float8_e4m3fn_x4
ALU = mybir.AluOpType
ACT = mybir.ActivationFunctionType

NT, NS, DH, DB = 1024, 4096, 1024, 256
EPS_ROW = 1e-8
EPS_BN = 1e-5

P = 128
PACK = 4
K_PASS = P * PACK
T_PASSES = NT // K_PASS
F_PASSES = DH // K_PASS
D_TILES = DB // P

SB = 512
ST = SB // P
NB = NS // SB
HB = SB // 2
HT = HB // P
SUM_COLS = 32
RUN = 4
N_RUN = 2

FLOPS = 2 * NS * NT * DH + 2 * NS * DH * DB


def tile_bipartitegcnstack_pb_t_kernel(
    tc, h_tgt, A, Wb0, bb0, bn_b_gamma, bn_b_beta, bn_b_mean, bn_b_var, out
):
    nc = tc.nc
    with ExitStack() as ctx:
        consts = ctx.enter_context(tc.tile_pool(name="consts", bufs=1))
        small = ctx.enter_context(tc.tile_pool(name="small", bufs=4))
        a_pool = ctx.enter_context(tc.tile_pool(name="a_pool", bufs=NB))
        h_pool = ctx.enter_context(tc.tile_pool(name="h_pool", bufs=F_PASSES * T_PASSES))
        hq_pool = ctx.enter_context(tc.tile_pool(name="hq_pool", bufs=F_PASSES * T_PASSES))
        w_pool = ctx.enter_context(tc.tile_pool(name="w_pool", bufs=1))
        an_pool = ctx.enter_context(tc.tile_pool(name="an_pool", bufs=4))
        aq_pool = ctx.enter_context(tc.tile_pool(name="aq_pool", bufs=6))
        gg_pool = ctx.enter_context(tc.tile_pool(name="gg_pool", bufs=4))
        gq_pool = ctx.enter_context(tc.tile_pool(name="gq_pool", bufs=6))
        act_pool = ctx.enter_context(tc.tile_pool(name="act_pool", bufs=2 * D_TILES))
        out_pool = ctx.enter_context(tc.tile_pool(name="out_pool", bufs=4))
        psum_sum = ctx.enter_context(tc.psum_pool(name="psum_sum", bufs=1))
        psum_inv = ctx.enter_context(tc.psum_pool(name="psum_inv", bufs=1))
        psum_agg = ctx.enter_context(tc.psum_pool(name="psum_agg", bufs=F_PASSES * HT))
        psum_post = ctx.enter_context(tc.psum_pool(name="psum_post", bufs=2))

        a_raw, h_raw = {}, {}
        sums, inv, inv_all = {}, {}, {}
        a_grp, agg_grp = {}, {}
        h_grp = {}
        a_q, agg_q, h_q = {}, {}, {}
        act_t = {}

        def regroup(copy, grouped, rows):
            copy(
                out=grouped.rearrange("p (q i) j -> p q j i", i=RUN),
                in_=rows.rearrange("p j (q i) -> p q j i", i=RUN),
            )

        def quantise(pool, label, grouped):
            width = grouped.shape[1]
            codes = pool.tile([P, width], U32, name=label + "_codes", align_bytes=64)
            scales = pool.tile([P, width], U8, name=label + "_scales", align_bytes=64)
            nc.vector.quantize_mx(
                out=codes[:].bitcast(FP8X4),
                scales=scales[:],
                in_=grouped[:].rearrange("p w j -> p (w j)"),
            )
            return codes, scales

        def load_a(b, first=0, width=SB):
            if first == 0:
                a_raw[b] = a_pool.tile([P, T_PASSES, PACK, SB], BF16, name="a_raw")
            for c in range(T_PASSES):
                rows = A[c * K_PASS : (c + 1) * K_PASS, b * SB + first : b * SB + first + width]
                nc.sync.dma_start(
                    out=a_raw[b][:, c, :, first : first + width],
                    in_=rows.rearrange("(p j) s -> p j s", j=PACK),
                )

        def load_h(g, c):
            h_raw[(g, c)] = h_pool.tile([P, PACK, K_PASS], BF16, name="h_raw")
            rows = h_tgt[c * K_PASS : (c + 1) * K_PASS, g * K_PASS : (g + 1) * K_PASS]
            nc.sync.dma_start(
                out=h_raw[(g, c)][:], in_=rows.rearrange("(p j) f -> p j f", j=PACK)
            )

        def regroup_h(copy, g, c):
            h_grp[(g, c)] = hq_pool.tile([P, K_PASS, PACK], BF16, name="h_grp", align_bytes=64)
            regroup(copy, h_grp[(g, c)][:], h_raw[(g, c)][:])

        def quantise_h(g, c):
            h_q[(g, c)] = quantise(hq_pool, "h", h_grp[(g, c)])

        def column_sums(b, tiles=range(ST)):
            if tiles[0] == 0:
                sums[b] = psum_sum.tile([P, ST, SUM_COLS], F32, name="sums", tag="sums")
            pieces = T_PASSES * PACK
            for st in tiles:
                for r in range(pieces):
                    nc.tensor.matmul(
                        out=sums[b][:, st, :],
                        lhsT=a_raw[b][:, r // PACK, r % PACK, st * P : (st + 1) * P],
                        rhs=ones[:],
                        start=(r == 0),
                        stop=(r == pieces - 1),
                    )

        def reciprocals(b, tiles=range(ST)):
            lo, hi = tiles[0], tiles[-1] + 1
            clamped = small.tile([P, ST], F32, name="clamped")
            nc.vector.tensor_scalar_max(
                out=clamped[:, lo:hi], in0=sums[b][:, lo:hi, 0], scalar1=EPS_ROW
            )
            if lo == 0:
                inv[b] = small.tile([P, ST], F32, name="inv")
            nc.vector.reciprocal(out=inv[b][:, lo:hi], in_=clamped[:, lo:hi])

        def spread(b, tiles=range(ST)):
            if tiles[0] == 0:
                inv_all[b] = psum_inv.tile([P, SB], F32, name="inv_all", tag="inv_all")
            for st in tiles:
                nc.tensor.transpose(
                    out=inv_all[b][:, st * P : (st + 1) * P],
                    in_=inv[b][:, st : st + 1].to_broadcast([P, P]),
                    identity=ident[:],
                )

        def normalise(b, half):
            nodes = slice(half * HB, (half + 1) * HB)
            a_grp[(b, half)] = an_pool.tile(
                [P, T_PASSES * HB, PACK], BF16, name="a_grp", align_bytes=64
            )
            for c in range(T_PASSES):
                nc.vector.tensor_tensor(
                    out=a_grp[(b, half)][:, c * HB : (c + 1) * HB, :].rearrange(
                        "p (q i) j -> p q j i", i=N_RUN
                    ),
                    in0=a_raw[b][:, c, :, nodes].rearrange("p j (q i) -> p q j i", i=N_RUN),
                    in1=inv_all[b][:, nodes]
                    .rearrange("p (q i) -> p q i", i=N_RUN)
                    .unsqueeze(2)
                    .to_broadcast([P, HB // N_RUN, PACK, N_RUN]),
                    op=ALU.mult,
                )

        def quantise_a(b, half):
            a_q[(b, half)] = quantise(aq_pool, "a", a_grp[(b, half)])

        def aggregate(b, half, passes=range(F_PASSES)):
            if passes[0] == 0:
                agg_grp[(b, half)] = gg_pool.tile(
                    [P, F_PASSES * HB, PACK], BF16, name="agg_grp", align_bytes=64
                )
            a_codes, a_scales = a_q[(b, half)]
            for g in passes:
                for k in range(HT):
                    bank = psum_agg.tile([P, PACK, P], F32, name="agg_bank", tag="agg_bank")
                    for i in range(PACK):
                        feats = slice(i * P, (i + 1) * P)
                        for c in range(T_PASSES):
                            nodes = slice(c * HB + k * P, c * HB + (k + 1) * P)
                            h_codes, h_scales = h_q[(g, c)]
                            nc.tensor.matmul_mx(
                                out=bank[:, i, :],
                                lhsT=h_codes[:, feats].bitcast(FP8X4),
                                lhsT_scale=h_scales[:, feats],
                                rhs=a_codes[:, nodes].bitcast(FP8X4),
                                rhs_scale=a_scales[:, nodes],
                                start=(c == 0),
                                stop=(c == T_PASSES - 1),
                            )
                    nc.scalar.copy(
                        out=agg_grp[(b, half)][:, g * HB + k * P : g * HB + (k + 1) * P, :],
                        in_=bank[:].rearrange("p i s -> p s i"),
                    )

        def quantise_agg(b, half):
            agg_q[(b, half)] = quantise(gq_pool, "agg", agg_grp[(b, half)])

        def free_bank(source):
            pool, tag = {
                "post": (psum_post, "post"),
                "agg": (psum_agg, "agg_bank"),
                "sum": (psum_sum, "sums"),
                "inv": (psum_inv, "inv_all"),
            }[source]
            return pool.tile([P, SB], F32, name="bank_" + source, tag=tag)

        def project(b, dt, halves=range(2), source="post"):
            bank = free_bank(source)
            w_codes, w_scales = w_q
            for half in halves:
                agg_codes, agg_scales = agg_q[(b, half)]
                for g in range(F_PASSES):
                    cols = slice(g * DB + dt * P, g * DB + (dt + 1) * P)
                    nodes = slice(g * HB, (g + 1) * HB)
                    nc.tensor.matmul_mx(
                        out=bank[:, half * HB : (half + 1) * HB],
                        lhsT=w_codes[:, cols].bitcast(FP8X4),
                        lhsT_scale=w_scales[:, cols],
                        rhs=agg_codes[:, nodes].bitcast(FP8X4),
                        rhs_scale=agg_scales[:, nodes],
                        start=(g == 0),
                        stop=(g == F_PASSES - 1),
                    )
            if halves[0] == 0:
                act_t[(b, dt)] = act_pool.tile([P, SB], F32, name="act_t")
            done = slice(halves[0] * HB, (halves[-1] + 1) * HB)
            nc.scalar.activation(
                out=act_t[(b, dt)][:, done],
                in_=bank[:, done],
                func=ACT.Relu,
                bias=bn_shift[:, dt : dt + 1],
                scale=bn_scale[:, dt : dt + 1],
            )

        def turn_and_store(b, pairs=range(ST // 2), copy=nc.scalar.copy, source="post"):
            for pair in pairs:
                bank = free_bank(source)
                for k in range(2):
                    nodes = slice((2 * pair + k) * P, (2 * pair + k + 1) * P)
                    for dt in range(D_TILES):
                        nc.tensor.transpose(
                            out=bank[:, k * DB + dt * P : k * DB + (dt + 1) * P],
                            in_=act_t[(b, dt)][:, nodes],
                            identity=ident[:],
                        )
                rows = out_pool.tile([P, 2, DB], F32, name="rows")
                copy(out=rows[:].rearrange("p k d -> p (k d)"), in_=bank[:])
                first = b * SB + 2 * pair * P
                nc.sync.dma_start(
                    out=out[first : first + 2 * P, :].rearrange("(k p) d -> p k d", p=P),
                    in_=rows[:],
                )

        def aggregate_tile(b, half, k):
            agg_grp[(b, half, k)] = gg_pool.tile(
                [P, F_PASSES * P, PACK], BF16, name="agg_grp", align_bytes=64
            )
            a_codes, a_scales = a_q[(b, half)]
            for g in range(F_PASSES):
                bank = psum_agg.tile([P, PACK, P], F32, name="agg_bank", tag="agg_bank")
                for i in range(PACK):
                    feats = slice(i * P, (i + 1) * P)
                    for c in range(T_PASSES):
                        nodes = slice(c * HB + k * P, c * HB + (k + 1) * P)
                        h_codes, h_scales = h_q[(g, c)]
                        nc.tensor.matmul_mx(
                            out=bank[:, i, :],
                            lhsT=h_codes[:, feats].bitcast(FP8X4),
                            lhsT_scale=h_scales[:, feats],
                            rhs=a_codes[:, nodes].bitcast(FP8X4),
                            rhs_scale=a_scales[:, nodes],
                            start=(c == 0),
                            stop=(c == T_PASSES - 1),
                        )
                nc.scalar.copy(
                    out=agg_grp[(b, half, k)][:, g * P : (g + 1) * P, :],
                    in_=bank[:].rearrange("p i s -> p s i"),
                )

        def quantise_agg_tile(b, half, k):
            agg_q[(b, half, k)] = quantise(gq_pool, "agg", agg_grp[(b, half, k)])

        def project_tile(b, half, k, sources):
            banks = [free_bank(source) for source in sources]
            w_codes, w_scales = w_q
            agg_codes, agg_scales = agg_q[(b, half, k)]
            act_k = act_pool.tile([P, D_TILES, P], F32, name="act_k")
            for dt in range(D_TILES):
                for g in range(F_PASSES):
                    cols = slice(g * DB + dt * P, g * DB + (dt + 1) * P)
                    nodes = slice(g * P, (g + 1) * P)
                    nc.tensor.matmul_mx(
                        out=banks[dt][:, 0:P],
                        lhsT=w_codes[:, cols].bitcast(FP8X4),
                        lhsT_scale=w_scales[:, cols],
                        rhs=agg_codes[:, nodes].bitcast(FP8X4),
                        rhs_scale=agg_scales[:, nodes],
                        start=(g == 0),
                        stop=(g == F_PASSES - 1),
                    )
            nc.scalar.activation(
                out=act_k[:, 0, :],
                in_=banks[0][:, 0:P],
                func=ACT.Relu,
                bias=bn_shift[:, 0:1],
                scale=bn_scale[:, 0:1],
            )
            nc.vector.tensor_scalar(
                out=act_k[:, 1, :],
                in0=banks[1][:, 0:P],
                scalar1=bn_scale[:, 1:2],
                scalar2=bn_shift[:, 1:2],
                op0=ALU.mult,
                op1=ALU.add,
            )
            return act_k

        def turn_tile(b, half, k, act_k, sources):
            banks = [free_bank(source) for source in sources]
            for dt in range(D_TILES):
                nc.tensor.transpose(out=banks[dt][:, 0:P], in_=act_k[:, dt, :], identity=ident[:])
            rows = out_pool.tile([P, DB], F32, name="rows_k")
            nc.scalar.copy(out=rows[:, 0:P], in_=banks[0][:, 0:P])
            nc.vector.tensor_scalar_max(out=rows[:, P:DB], in0=banks[1][:, 0:P], scalar1=0.0)
            first = b * SB + (half * HT + k) * P
            nc.sync.dma_start(out=out[first : first + P, :], in_=rows[:])

        ident = consts.tile([P, P], F32, name="ident")
        make_identity(nc, ident[:])
        ident_bf = consts.tile([P, P], BF16, name="ident_bf")
        make_identity(nc, ident_bf[:])
        ones = consts.tile([P, SUM_COLS], BF16, name="ones")
        nc.vector.memset(ones[:], 1.0)

        vectors = [bb0, bn_b_gamma, bn_b_beta, bn_b_mean, bn_b_var]
        vec_rows = consts.tile([P, P], BF16, name="vec_rows")
        nc.vector.memset(vec_rows[:], 0.0)
        for v in range(len(vectors)):
            nc.scalar.dma_start(
                out=vec_rows[v * D_TILES : (v + 1) * D_TILES, :],
                in_=vectors[v].rearrange("(dt d) -> dt d", dt=D_TILES),
            )

        load_h(0, 0)
        load_a(0, 0, HB)
        load_h(0, 1)
        load_h(1, 0)
        load_h(1, 1)
        load_a(0, HB, HB)
        load_a(1)
        w_raw = w_pool.tile([P, F_PASSES * PACK, DB], BF16, name="w_raw")
        nc.sync.dma_start(out=w_raw[:], in_=Wb0.rearrange("(gi p) d -> p gi d", p=P))
        for b in range(2, NB):
            load_a(b)

        warm = consts.tile([P, 1], F32, name="warm")
        nc.scalar.activation(out=warm[:], in_=ones[:, 0:1], func=ACT.Sqrt)
        first_half, second_half = range(0, HT), range(HT, ST)
        pass_0, pass_1 = range(0, 1), range(1, 2)
        regroup_h(nc.vector.tensor_copy, 0, 0)
        column_sums(0, first_half)
        quantise_h(0, 0)
        reciprocals(0, first_half)
        spread(0, first_half)
        regroup_h(nc.scalar.copy, 0, 1)
        normalise(0, 0)
        regroup_h(nc.scalar.copy, 1, 0)
        quantise_h(0, 1)
        quantise_a(0, 0)
        column_sums(0, second_half)
        vec_bank = psum_post.tile([P, P], BF16, name="vec_bank", tag="post")
        nc.tensor.transpose(out=vec_bank[:], in_=vec_rows[:], identity=ident_bf[:])
        kept = len(vectors) - 1
        vec_t = consts.tile([P, kept, D_TILES], F32, name="vec_t")
        nc.scalar.copy(
            out=vec_t[:].rearrange("p v dt -> p (v dt)"), in_=vec_bank[:, 0 : kept * D_TILES]
        )
        bias_t, gamma_t, beta_t, mean_t = [vec_t[:, v, :] for v in range(kept)]
        std = consts.tile([P, D_TILES], F32, name="std")
        nc.scalar.activation(
            out=std[:],
            in_=vec_bank[:, kept * D_TILES : (kept + 1) * D_TILES],
            func=ACT.Sqrt,
            bias=EPS_BN,
        )
        aggregate(0, 0, pass_0)
        regroup_h(nc.vector.tensor_copy, 1, 1)
        reciprocals(0, second_half)
        spread(0, second_half)
        quantise_h(1, 0)
        quantise_h(1, 1)
        column_sums(1)
        aggregate(0, 0, pass_1)
        normalise(0, 1)
        rstd = consts.tile([P, D_TILES], F32, name="rstd")
        nc.vector.reciprocal(out=rstd[:], in_=std[:])
        bn_scale = consts.tile([P, D_TILES], F32, name="bn_scale")
        nc.gpsimd.tensor_tensor(out=bn_scale[:], in0=gamma_t, in1=rstd[:], op=ALU.mult)
        centred = consts.tile([P, D_TILES], F32, name="centred")
        nc.gpsimd.tensor_tensor(out=centred[:], in0=bias_t, in1=mean_t, op=ALU.subtract)
        scaled = consts.tile([P, D_TILES], F32, name="scaled")
        nc.gpsimd.tensor_tensor(out=scaled[:], in0=centred[:], in1=bn_scale[:], op=ALU.mult)
        bn_shift = consts.tile([P, D_TILES], F32, name="bn_shift")
        nc.gpsimd.tensor_tensor(out=bn_shift[:], in0=scaled[:], in1=beta_t, op=ALU.add)

        reciprocals(1)
        quantise_a(0, 1)
        spread(1)
        w_grp = w_pool.tile([P, F_PASSES * DB, PACK], BF16, name="w_grp", align_bytes=64)
        for g in range(F_PASSES):
            regroup(
                nc.scalar.copy,
                w_grp[:, g * DB : (g + 1) * DB, :],
                w_raw[:, g * PACK : (g + 1) * PACK, :],
            )
        normalise(1, 0)
        column_sums(2)
        reciprocals(2)
        quantise_agg(0, 0)
        quantise_a(1, 0)
        w_q = quantise(w_pool, "w", w_grp)
        aggregate(0, 1)

        last = NB - 1
        for b in range(1, NB):
            normalise(b, 1)
            quantise_agg(b - 1, 1)
            quantise_a(b, 1)
            aggregate(b, 0)
            if b + 1 < NB:
                spread(b + 1)
            if b >= 2:
                turn_and_store(b - 2)
            if b + 1 < NB:
                normalise(b + 1, 0)
            if b + 2 < NB:
                column_sums(b + 2)
                reciprocals(b + 2)
            project(b - 1, 0, source="post" if b + 2 < NB else "sum")
            project(b - 1, 1, source="post" if b < last else "inv")
            quantise_agg(b, 0)
            if b + 1 < NB:
                quantise_a(b + 1, 0)
            if b < last:
                aggregate(b, 1)

        aggregate_tile(last, 1, 0)
        aggregate_tile(last, 1, 1)
        quantise_agg_tile(last, 1, 0)
        project(last, 0, range(0, 1), source="sum")
        project(last, 1, range(0, 1), source="inv")
        quantise_agg_tile(last, 1, 1)
        act_0 = project_tile(last, 1, 0, ["agg", "agg"])
        turn_and_store(last - 1, copy=nc.vector.tensor_copy)
        act_1 = project_tile(last, 1, 1, ["agg", "agg"])
        turn_and_store(last, range(0, 1), source="sum")
        turn_tile(last, 1, 0, act_0, ["inv", "agg"])
        turn_tile(last, 1, 1, act_1, ["post", "post"])
